import numpy as np
import ml_dtypes


def mxq(x, axis, fmt="e4m3"):
    dtype, down = {"e4m3": (ml_dtypes.float8_e4m3fn, 7), "e5m2": (ml_dtypes.float8_e5m2, 14)}[fmt]
    v = np.moveaxis(np.asarray(x, np.float32).astype(ml_dtypes.bfloat16).astype(np.float64), axis, -1)
    blocks = v.reshape(v.shape[:-1] + (-1, 32))
    amax = np.abs(blocks).max(-1, keepdims=True)
    byte = np.maximum(np.where(amax > 0, np.frexp(amax)[1] - 1 + 127, 0) - down, 1)
    scale = np.exp2(byte - 127.0)
    codes = (blocks / scale).astype(np.float32).astype(dtype).astype(np.float64)
    return np.moveaxis((codes * scale).reshape(v.shape), -1, axis)


WIDE = False


def mx_kscale(k):
    if not WIDE:
        return np.ones(k)
    levels = np.array([10, -10, 5, -5, 0])
    a = np.random.permutation(np.resize(levels, k // 512 * 4)).reshape(k // 512, 4)
    idx = np.arange(k)
    return np.exp2(a[idx // 512, idx % 128 // 32])


BF16 = ml_dtypes.bfloat16


def bf(x):
    return np.asarray(x, np.float32).astype(BF16)


def f64(x):
    return np.asarray(x).astype(np.float64)


E2M1 = np.array([0.0, 0.5, 1.0, 1.5, 2.0, 3.0, 4.0, 6.0, -0.0, -0.5, -1.0, -1.5, -2.0, -3.0, -4.0, -6.0])


def pack_weight(w, fmt):
    k, n = w.shape
    w = f64(bf(w)).reshape(k // 32, 32, n)
    amax = np.abs(w).max(1)
    if fmt == "e4m3":
        byte = np.frexp(amax)[1] - 1 + 127 - 7
    else:
        mant, ex = np.frexp(amax / 6.0)
        byte = np.where(mant > 0.5, ex, ex - 1) + 127
    byte = np.clip(np.where(amax > 0, byte, 1), 1, 254)
    scaled = (w * np.exp2(127.0 - byte)[:, None, :]).reshape(k, n).astype(np.float32)
    by_word = np.ascontiguousarray(scaled.reshape(k // 512, 128, 4, n).transpose(0, 1, 3, 2))
    if fmt == "e4m3":
        words = by_word.astype(ml_dtypes.float8_e4m3fn).view(np.uint8)
    else:
        c = by_word.astype(ml_dtypes.float4_e2m1fn).view(np.uint8) & 0xF
        words = c[..., 0::2] | (c[..., 1::2] << 4)
    return np.ascontiguousarray(words), np.ascontiguousarray(byte.astype(np.uint8).reshape(k // 512, 16, n))


def unpack_weight(words, scales, fmt):
    g, p, n, _ = words.shape
    if fmt == "e4m3":
        vals = np.ascontiguousarray(words).view(ml_dtypes.float8_e4m3fn).astype(np.float64)
    else:
        nib = np.empty((g, p, n, 4), np.uint8)
        nib[..., 0::2] = words & 0xF
        nib[..., 1::2] = words >> 4
        vals = E2M1[nib]
    vals = vals * np.repeat(np.exp2(scales.astype(np.float64) - 127.0), 8, axis=1)[..., None]
    return vals.transpose(0, 1, 3, 2).reshape(g * 512, n)


B, N, E, H, G, D, WIN = 1, 128, 16384, 8, 4, 128, 512
HK = H // G
HALF = D // 2
FMT = "e4m3"


def apply_rope(y, cos, sin):
    By, Ny, Hy, Dy = y.shape
    yp = y.reshape(By, Ny, Hy, Dy // 2, 2)
    y0, y1 = yp[..., 0], yp[..., 1]
    c = cos[:, :, None, :]
    s = sin[:, :, None, :]
    r0 = y0 * c - y1 * s
    r1 = y0 * s + y1 * c
    return np.stack([r0, r1], axis=-1).reshape(By, Ny, Hy, Dy)


def setup_inputs():
    s = mx_kscale(E)
    inv_freq = 1.0 / 10000.0 ** (np.arange(HALF) / HALF)
    ang = np.arange(N)[:, None] * inv_freq[None, :]
    x = bf(np.random.standard_normal((B, N, E)) * s)
    rope_cos = bf(np.broadcast_to(np.cos(ang)[None], (B, N, HALF)))
    rope_sin = bf(np.broadcast_to(np.sin(ang)[None], (B, N, HALF)))
    Wq_words, Wq_scales = pack_weight(np.random.standard_normal((E, H * D)) * 1.5 / np.sqrt(E) / s[:, None], FMT)
    Wk_words, Wk_scales = pack_weight(np.random.standard_normal((E, HK * D)) * 1.5 / np.sqrt(E) / s[:, None], FMT)
    Wv_words, Wv_scales = pack_weight(np.random.standard_normal((E, HK * D)) / np.sqrt(E) / s[:, None], FMT)
    return {"x": x,
            "rope_cos": rope_cos,
            "rope_sin": rope_sin,
            "Wq_words": Wq_words, "Wq_scales": Wq_scales,
            "Wk_words": Wk_words, "Wk_scales": Wk_scales,
            "Wv_words": Wv_words, "Wv_scales": Wv_scales}


def reference(x, rope_cos, rope_sin, Wq_words, Wq_scales, Wk_words, Wk_scales, Wv_words, Wv_scales):
    xq = mxq(f64(x), 2, "e4m3")
    q = (xq @ unpack_weight(Wq_words, Wq_scales, FMT)).reshape(B, N, H, D)
    k = (xq @ unpack_weight(Wk_words, Wk_scales, FMT)).reshape(B, N, HK, D)
    v = (xq @ unpack_weight(Wv_words, Wv_scales, FMT)).reshape(B, N, HK, D)
    q = apply_rope(q, f64(rope_cos), f64(rope_sin))
    k = apply_rope(k, f64(rope_cos), f64(rope_sin))
    return q.transpose(0, 2, 1, 3), k.transpose(0, 2, 1, 3), v.transpose(0, 2, 1, 3)

@@ -1,0 +1,221 @@
+from contextlib import ExitStack
+
+import concourse.mybir as mybir
+from concourse.masks import make_identity
+
+F32 = mybir.dt.float32
+BF16 = mybir.dt.bfloat16
+I32 = mybir.dt.int32
+U32 = mybir.dt.uint32
+U8 = mybir.dt.uint8
+FP8X4 = mybir.dt.float8_e4m3fn_x4
+MULT = mybir.AluOpType.mult
+ADD = mybir.AluOpType.add
+
+P = 128
+E = 16384
+K_PASS = 512
+GROUPS = E // K_PASS
+D = 128
+HALF = D // 2
+Q_COLS, K_COLS, V_COLS = 1024, 256, 256
+BANK = 512
+PLANES = 4
+
+CHUNK_WORDS = 2048
+CHUNK_BUFS = 16
+X_CHUNKS = 4
+X_CHUNK_GROUPS = GROUPS // X_CHUNKS
+QUANT_GROUPS = 4
+
+FLOPS = 2 * P * E * (Q_COLS + K_COLS + V_COLS)
+
+
+def tile_groupedqueryattention_pa_k_kernel(
+    tc, x, rope_cos, rope_sin,
+    Wq_words, Wq_scales, Wk_words, Wk_scales, Wv_words, Wv_scales,
+    out_0, out_1, out_2,
+):
+    nc = tc.nc
+    with ExitStack() as ctx:
+        ctx.enter_context(tc.manual_schedule())
+        keep = ctx.enter_context(tc.tile_pool(name="keep", bufs=1))
+        x_in = ctx.enter_context(tc.tile_pool(name="x_in", bufs=X_CHUNKS))
+        stage = ctx.enter_context(tc.tile_pool(name="stage", bufs=3))
+        weights = ctx.enter_context(tc.tile_pool(name="weights", bufs=CHUNK_BUFS))
+        work = ctx.enter_context(tc.tile_pool(name="work", bufs=2))
+        flip = ctx.enter_context(tc.psum_pool(name="flip", bufs=4))
+        sums = ctx.enter_context(tc.psum_pool(name="sums", bufs=1))
+
+        def projection(name, words, scales, cols):
+            planes = keep.tile([P, GROUPS // PLANES, cols], U8, name=name + "_planes", align_bytes=64)
+            nc.vector.memset(planes[:].bitcast(I32), 0)
+            width = min(cols, BANK)
+            banks = [
+                sums.tile([P, width], F32, name="%s_sum%d" % (name, b)) for b in range(cols // width)
+            ]
+            return {
+                "words": words.rearrange("g p n t -> g p (n t)").bitcast(I32),
+                "scales": scales.bitcast(I32),
+                "planes": planes,
+                "cols": cols,
+                "width": width,
+                "banks": banks,
+                "groups_per_chunk": CHUNK_WORDS // cols,
+            }
+
+        proj_q = projection("q", Wq_words, Wq_scales, Q_COLS)
+        proj_k = projection("k", Wk_words, Wk_scales, K_COLS)
+        proj_v = projection("v", Wv_words, Wv_scales, V_COLS)
+
+        identity = keep.tile([P, P], F32, name="identity")
+        make_identity(nc, identity[:])
+
+        x_tiles = []
+        for c in range(X_CHUNKS):
+            x_tile = x_in.tile([P, E // X_CHUNKS], BF16, name="x_tile")
+            nc.sync.dma_start(out=x_tile[:], in_=x[0, :, c * (E // X_CHUNKS) : (c + 1) * (E // X_CHUNKS)])
+            x_tiles.append(x_tile)
+
+        cos_bf = keep.tile([P, HALF], BF16, name="cos_bf")
+        sin_bf = keep.tile([P, HALF], BF16, name="sin_bf")
+        nc.scalar.dma_start(out=cos_bf[:], in_=rope_cos[0])
+        nc.scalar.dma_start(out=sin_bf[:], in_=rope_sin[0])
+
+        def load_scales(proj):
+            plane_words = proj["planes"][:].bitcast(I32)
+            for quadrant in range(4):
+                for r in range(4):
+                    first = 32 * quadrant + r
+                    nc.sync.dma_start(
+                        out=plane_words[first : first + 4 * PLANES : 4, :, :],
+                        in_=proj["scales"][:, 4 * quadrant + r, :].rearrange("(a j) w -> j a w", j=PLANES),
+                    )
+
+        def load_chunk(proj, first_group):
+            n_groups = proj["groups_per_chunk"]
+            chunk = weights.tile([P, CHUNK_WORDS], I32, name="chunk", align_bytes=64)
+            nc.sync.dma_start(
+                out=chunk[:].rearrange("p (g w) -> p g w", g=n_groups),
+                in_=proj["words"][first_group : first_group + n_groups].rearrange("g p w -> p g w"),
+            )
+            return chunk
+
+        stream = []
+        for proj in (proj_q, proj_k, proj_v):
+            for first_group in range(0, GROUPS, proj["groups_per_chunk"]):
+                stream.append((proj, first_group))
+
+        load_scales(proj_q)
+        chunks = [load_chunk(proj, first_group) for proj, first_group in stream[:CHUNK_BUFS]]
+        load_scales(proj_k)
+        load_scales(proj_v)
+
+        x_codes = keep.tile([P, GROUPS * P], U32, name="x_codes", align_bytes=64)
+        x_planes = keep.tile([P, GROUPS * P], U8, name="x_planes", align_bytes=64)
+
+        def regroup(first_group):
+            grouped = stage.tile([P, QUANT_GROUPS, P, 4], BF16, name="grouped", align_bytes=64)
+            grouped_words = grouped[:].bitcast(F32)
+            for half in range(QUANT_GROUPS // 2):
+                flipped = flip.tile([P, 2, 2, P], F32, name="flipped")
+                for i in range(2):
+                    g = first_group + 2 * half + i
+                    x_words = x_tiles[g // X_CHUNK_GROUPS][:].bitcast(F32)
+                    base = (K_PASS // 2) * (g % X_CHUNK_GROUPS)
+                    for u in range(2):
+                        nc.tensor.transpose(
+                            flipped[:, i, u, :], x_words[:, base + u : base + K_PASS // 2 : 2], identity[:]
+                        )
+                copy = nc.vector.tensor_copy if half % 2 == 0 else nc.scalar.copy
+                copy(
+                    out=grouped_words[:, 2 * half : 2 * half + 2, :, :],
+                    in_=flipped[:].rearrange("p i u m -> p i m u"),
+                )
+            return grouped
+
+        def quantise(grouped, first_group):
+            cols = slice(first_group * P, (first_group + QUANT_GROUPS) * P)
+            nc.vector.quantize_mx(
+                out=x_codes[:, cols].bitcast(FP8X4),
+                scales=x_planes[:, cols],
+                in_=grouped[:].rearrange("p g m t -> p (g m t)"),
+            )
+
+        waiting = None
+        for first_group in range(0, GROUPS, QUANT_GROUPS):
+            grouped = regroup(first_group)
+            if waiting is not None:
+                quantise(waiting[0], waiting[1])
+            waiting = (grouped, first_group)
+        quantise(waiting[0], waiting[1])
+
+        cos_pair = keep.tile([P, HALF, 2], F32, name="cos_pair")
+        sin_minus = keep.tile([P, HALF], F32, name="sin_minus")
+        sin_plus = keep.tile([P, HALF], F32, name="sin_plus")
+        nc.vector.tensor_copy(out=cos_pair[:], in_=cos_bf[:].unsqueeze(2).to_broadcast([P, HALF, 2]))
+        nc.vector.tensor_copy(out=sin_plus[:], in_=sin_bf[:])
+        nc.vector.tensor_scalar_mul(out=sin_minus[:], in0=sin_bf[:], scalar1=-1.0)
+
+        def rotate_and_store(bank, out_heads):
+            heads = out_heads.shape[0]
+            y = bank[:].rearrange("p (h q e) -> p h q e", h=heads, e=2)
+            by_cos = work.tile([P, heads, D], F32, name="by_cos")
+            nc.vector.tensor_tensor(
+                out=by_cos[:],
+                in0=bank[:].rearrange("p (h d) -> p h d", h=heads),
+                in1=cos_pair[:].rearrange("p q e -> p (q e)").unsqueeze(1).to_broadcast([P, heads, D]),
+                op=MULT,
+            )
+            by_sin = work.tile([P, 2, heads, HALF], F32, name="by_sin")
+            nc.vector.tensor_tensor(
+                out=by_sin[:, 0], in0=y[:, :, :, 1],
+                in1=sin_minus[:].unsqueeze(1).to_broadcast([P, heads, HALF]), op=MULT,
+            )
+            nc.vector.tensor_tensor(
+                out=by_sin[:, 1], in0=y[:, :, :, 0],
+                in1=sin_plus[:].unsqueeze(1).to_broadcast([P, heads, HALF]), op=MULT,
+            )
+            rotated = work.tile([P, heads, HALF, 2], F32, name="rotated")
+            nc.vector.tensor_tensor(
+                out=rotated[:],
+                in0=by_cos[:].rearrange("p h (q e) -> p h q e", e=2),
+                in1=by_sin[:].rearrange("p e h q -> p h q e"),
+                op=ADD,
+            )
+            nc.scalar.dma_start(
+                out=out_heads.rearrange("h n d -> n h d"),
+                in_=rotated[:].rearrange("p h q e -> p h (q e)"),
+            )
+
+        for index, (proj, first_group) in enumerate(stream):
+            chunk = chunks[index]
+            cols, width = proj["cols"], proj["width"]
+            for i in range(proj["groups_per_chunk"]):
+                g = first_group + i
+                for b, bank in enumerate(proj["banks"]):
+                    nc.tensor.matmul_mx(
+                        out=bank[:],
+                        lhsT=x_codes[:, g * P : (g + 1) * P].bitcast(FP8X4),
+                        lhsT_scale=x_planes[:, g * P : (g + 1) * P],
+                        rhs=chunk[:, i * cols + b * width : i * cols + (b + 1) * width].bitcast(FP8X4),
+                        rhs_scale=proj["planes"][4 * (g % PLANES) : P, g // PLANES, b * width : (b + 1) * width],
+                        start=(g == 0),
+                        stop=(g == GROUPS - 1),
+                    )
+            if index + CHUNK_BUFS < len(stream):
+                chunks.append(load_chunk(stream[index + CHUNK_BUFS][0], stream[index + CHUNK_BUFS][1]))
+            if first_group + proj["groups_per_chunk"] == GROUPS:
+                if proj is proj_q:
+                    heads_a_bank = BANK // D
+                    for b, bank in enumerate(proj["banks"]):
+                        rotate_and_store(bank, out_0[0, b * heads_a_bank : (b + 1) * heads_a_bank])
+                elif proj is proj_k:
+                    rotate_and_store(proj["banks"][0], out_1[0])
+                else:
+                    v_rows = work.tile([P, V_COLS], F32, name="v_rows")
+                    nc.vector.tensor_copy(out=v_rows[:], in_=proj["banks"][0][:])
+                    nc.sync.dma_start(
+                        out=out_2[0].rearrange("h n d -> n h d"),
+                        in_=v_rows[:].rearrange("p (h d) -> p h d", d=D),
+                    )

@@ -56,7 +56,7 @@ def tile_groupedqueryattention_pa_k_kernel(
             ]
             return {
                 "words": words.rearrange("g p n t -> g p (n t)").bitcast(I32),
-                "scales": scales.bitcast(I32),
+                "scales": scales.bitcast(F32),
                 "planes": planes,
                 "cols": cols,
                 "width": width,
@@ -83,11 +83,11 @@ def tile_groupedqueryattention_pa_k_kernel(
         nc.scalar.dma_start(out=sin_bf[:], in_=rope_sin[0])
 
         def load_scales(proj):
-            plane_words = proj["planes"][:].bitcast(I32)
+            plane_words = proj["planes"][:].bitcast(F32)
             for quadrant in range(4):
                 for r in range(4):
                     first = 32 * quadrant + r
-                    nc.sync.dma_start(
+                    nc.gpsimd.dma_start(
                         out=plane_words[first : first + 4 * PLANES : 4, :, :],
                         in_=proj["scales"][:, 4 * quadrant + r, :].rearrange("(a j) w -> j a w", j=PLANES),
                     )

@@ -20,10 +20,9 @@ D = 128
 HALF = D // 2
 Q_COLS, K_COLS, V_COLS = 1024, 256, 256
 BANK = 512
-PLANES = 4
 
 CHUNK_WORDS = 2048
-CHUNK_BUFS = 16
+CHUNK_BUFS = 13
 X_CHUNKS = 4
 X_CHUNK_GROUPS = GROUPS // X_CHUNKS
 QUANT_GROUPS = 4
@@ -47,8 +46,8 @@ def tile_groupedqueryattention_pa_k_kernel(
         flip = ctx.enter_context(tc.psum_pool(name="flip", bufs=4))
         sums = ctx.enter_context(tc.psum_pool(name="sums", bufs=1))
 
-        def projection(name, words, scales, cols):
-            planes = keep.tile([P, GROUPS // PLANES, cols], U8, name=name + "_planes", align_bytes=64)
+        def projection(name, words, scales, cols, offsets):
+            planes = keep.tile([P, GROUPS // len(offsets), cols], U8, name=name + "_planes", align_bytes=64)
             nc.vector.memset(planes[:].bitcast(I32), 0)
             width = min(cols, BANK)
             banks = [
@@ -58,15 +57,16 @@ def tile_groupedqueryattention_pa_k_kernel(
                 "words": words.rearrange("g p n t -> g p (n t)").bitcast(I32),
                 "scales": scales.bitcast(F32),
                 "planes": planes,
+                "offsets": offsets,
                 "cols": cols,
                 "width": width,
                 "banks": banks,
                 "groups_per_chunk": CHUNK_WORDS // cols,
             }
 
-        proj_q = projection("q", Wq_words, Wq_scales, Q_COLS)
-        proj_k = projection("k", Wk_words, Wk_scales, K_COLS)
-        proj_v = projection("v", Wv_words, Wv_scales, V_COLS)
+        proj_q = projection("q", Wq_words, Wq_scales, Q_COLS, (0, 12))
+        proj_k = projection("k", Wk_words, Wk_scales, K_COLS, (4,))
+        proj_v = projection("v", Wv_words, Wv_scales, V_COLS, (8,))
 
         identity = keep.tile([P, P], F32, name="identity")
         make_identity(nc, identity[:])
@@ -84,13 +84,10 @@ def tile_groupedqueryattention_pa_k_kernel(
 
         def load_scales(proj):
             plane_words = proj["planes"][:].bitcast(F32)
-            for quadrant in range(4):
+            by_row = proj["scales"].rearrange("(a j) (q r) w -> j r q a w", j=len(proj["offsets"]), r=4)
+            for j, offset in enumerate(proj["offsets"]):
                 for r in range(4):
-                    first = 32 * quadrant + r
-                    nc.gpsimd.dma_start(
-                        out=plane_words[first : first + 4 * PLANES : 4, :, :],
-                        in_=proj["scales"][:, 4 * quadrant + r, :].rearrange("(a j) w -> j a w", j=PLANES),
-                    )
+                    nc.gpsimd.dma_start(out=plane_words[offset + r : P : 32, :, :], in_=by_row[j, r])
 
         def load_chunk(proj, first_group):
             n_groups = proj["groups_per_chunk"]
@@ -190,7 +187,7 @@ def tile_groupedqueryattention_pa_k_kernel(
 
         for index, (proj, first_group) in enumerate(stream):
             chunk = chunks[index]
-            cols, width = proj["cols"], proj["width"]
+            cols, width, offsets = proj["cols"], proj["width"], proj["offsets"]
             for i in range(proj["groups_per_chunk"]):
                 g = first_group + i
                 for b, bank in enumerate(proj["banks"]):
@@ -199,7 +196,9 @@ def tile_groupedqueryattention_pa_k_kernel(
                         lhsT=x_codes[:, g * P : (g + 1) * P].bitcast(FP8X4),
                         lhsT_scale=x_planes[:, g * P : (g + 1) * P],
                         rhs=chunk[:, i * cols + b * width : i * cols + (b + 1) * width].bitcast(FP8X4),
-                        rhs_scale=proj["planes"][4 * (g % PLANES) : P, g // PLANES, b * width : (b + 1) * width],
+                        rhs_scale=proj["planes"][
+                            offsets[g % len(offsets)] : P, g // len(offsets), b * width : (b + 1) * width
+                        ],
                         start=(g == 0),
                         stop=(g == GROUPS - 1),
                     )

@@ -20,9 +20,11 @@ D = 128
 HALF = D // 2
 Q_COLS, K_COLS, V_COLS = 1024, 256, 256
 BANK = 512
+PLANES = 4
 
 CHUNK_WORDS = 2048
-CHUNK_BUFS = 13
+MAX_RUNS = 4
+CHUNK_BUFS = 16
 X_CHUNKS = 4
 X_CHUNK_GROUPS = GROUPS // X_CHUNKS
 QUANT_GROUPS = 4
@@ -46,8 +48,8 @@ def tile_groupedqueryattention_pa_k_kernel(
         flip = ctx.enter_context(tc.psum_pool(name="flip", bufs=4))
         sums = ctx.enter_context(tc.psum_pool(name="sums", bufs=1))
 
-        def projection(name, words, scales, cols, offsets):
-            planes = keep.tile([P, GROUPS // len(offsets), cols], U8, name=name + "_planes", align_bytes=64)
+        def projection(name, words, scales, cols):
+            planes = keep.tile([P, GROUPS // PLANES, cols], U8, name=name + "_planes", align_bytes=64)
             nc.vector.memset(planes[:].bitcast(I32), 0)
             width = min(cols, BANK)
             banks = [
@@ -57,16 +59,15 @@ def tile_groupedqueryattention_pa_k_kernel(
                 "words": words.rearrange("g p n t -> g p (n t)").bitcast(I32),
                 "scales": scales.bitcast(F32),
                 "planes": planes,
-                "offsets": offsets,
                 "cols": cols,
                 "width": width,
                 "banks": banks,
-                "groups_per_chunk": CHUNK_WORDS // cols,
+                "groups_per_chunk": min(CHUNK_WORDS // cols, MAX_RUNS),
             }
 
-        proj_q = projection("q", Wq_words, Wq_scales, Q_COLS, (0, 12))
-        proj_k = projection("k", Wk_words, Wk_scales, K_COLS, (4,))
-        proj_v = projection("v", Wv_words, Wv_scales, V_COLS, (8,))
+        proj_q = projection("q", Wq_words, Wq_scales, Q_COLS)
+        proj_k = projection("k", Wk_words, Wk_scales, K_COLS)
+        proj_v = projection("v", Wv_words, Wv_scales, V_COLS)
 
         identity = keep.tile([P, P], F32, name="identity")
         make_identity(nc, identity[:])
@@ -84,16 +85,18 @@ def tile_groupedqueryattention_pa_k_kernel(
 
         def load_scales(proj):
             plane_words = proj["planes"][:].bitcast(F32)
-            by_row = proj["scales"].rearrange("(a j) (q r) w -> j r q a w", j=len(proj["offsets"]), r=4)
-            for j, offset in enumerate(proj["offsets"]):
+            for quadrant in range(4):
                 for r in range(4):
-                    nc.gpsimd.dma_start(out=plane_words[offset + r : P : 32, :, :], in_=by_row[j, r])
+                    first = 32 * quadrant + r
+                    nc.gpsimd.dma_start(
+                        out=plane_words[first : first + 4 * PLANES : 4, :, :],
+                        in_=proj["scales"][:, 4 * quadrant + r, :].rearrange("(a j) w -> j a w", j=PLANES),
+                    )
 
-        def load_chunk(proj, first_group):
-            n_groups = proj["groups_per_chunk"]
+        def load_chunk(proj, first_group, n_groups):
             chunk = weights.tile([P, CHUNK_WORDS], I32, name="chunk", align_bytes=64)
             nc.sync.dma_start(
-                out=chunk[:].rearrange("p (g w) -> p g w", g=n_groups),
+                out=chunk[:, : n_groups * proj["cols"]].rearrange("p (g w) -> p g w", g=n_groups),
                 in_=proj["words"][first_group : first_group + n_groups].rearrange("g p w -> p g w"),
             )
             return chunk
@@ -101,10 +104,13 @@ def tile_groupedqueryattention_pa_k_kernel(
         stream = []
         for proj in (proj_q, proj_k, proj_v):
             for first_group in range(0, GROUPS, proj["groups_per_chunk"]):
-                stream.append((proj, first_group))
+                stream.append((proj, first_group, proj["groups_per_chunk"]))
+        proj, first_group, n_groups = stream[-1]
+        stream[-1] = (proj, first_group, n_groups // 2)
+        stream.append((proj, first_group + n_groups // 2, n_groups // 2))
 
         load_scales(proj_q)
-        chunks = [load_chunk(proj, first_group) for proj, first_group in stream[:CHUNK_BUFS]]
+        chunks = [load_chunk(proj, first_group, n_groups) for proj, first_group, n_groups in stream[:CHUNK_BUFS]]
         load_scales(proj_k)
         load_scales(proj_v)
 
@@ -185,10 +191,10 @@ def tile_groupedqueryattention_pa_k_kernel(
                 in_=rotated[:].rearrange("p h q e -> p h (q e)"),
             )
 
-        for index, (proj, first_group) in enumerate(stream):
+        for index, (proj, first_group, n_groups) in enumerate(stream):
             chunk = chunks[index]
-            cols, width, offsets = proj["cols"], proj["width"], proj["offsets"]
-            for i in range(proj["groups_per_chunk"]):
+            cols, width = proj["cols"], proj["width"]
+            for i in range(n_groups):
                 g = first_group + i
                 for b, bank in enumerate(proj["banks"]):
                     nc.tensor.matmul_mx(
@@ -196,15 +202,14 @@ def tile_groupedqueryattention_pa_k_kernel(
                         lhsT=x_codes[:, g * P : (g + 1) * P].bitcast(FP8X4),
                         lhsT_scale=x_planes[:, g * P : (g + 1) * P],
                         rhs=chunk[:, i * cols + b * width : i * cols + (b + 1) * width].bitcast(FP8X4),
-                        rhs_scale=proj["planes"][
-                            offsets[g % len(offsets)] : P, g // len(offsets), b * width : (b + 1) * width
-                        ],
+                        rhs_scale=proj["planes"][4 * (g % PLANES) : P, g // PLANES, b * width : (b + 1) * width],
                         start=(g == 0),
                         stop=(g == GROUPS - 1),
                     )
             if index + CHUNK_BUFS < len(stream):
-                chunks.append(load_chunk(stream[index + CHUNK_BUFS][0], stream[index + CHUNK_BUFS][1]))
-            if first_group + proj["groups_per_chunk"] == GROUPS:
+                later = stream[index + CHUNK_BUFS]
+                chunks.append(load_chunk(later[0], later[1], later[2]))
+            if first_group + n_groups == GROUPS:
                 if proj is proj_q:
                     heads_a_bank = BANK // D
                     for b, bank in enumerate(proj["banks"]):

@@ -83,12 +83,12 @@ def tile_groupedqueryattention_pa_k_kernel(
         nc.scalar.dma_start(out=cos_bf[:], in_=rope_cos[0])
         nc.scalar.dma_start(out=sin_bf[:], in_=rope_sin[0])
 
-        def load_scales(proj):
+        def load_scales(proj, queue):
             plane_words = proj["planes"][:].bitcast(F32)
             for quadrant in range(4):
                 for r in range(4):
                     first = 32 * quadrant + r
-                    nc.gpsimd.dma_start(
+                    queue.dma_start(
                         out=plane_words[first : first + 4 * PLANES : 4, :, :],
                         in_=proj["scales"][:, 4 * quadrant + r, :].rearrange("(a j) w -> j a w", j=PLANES),
                     )
@@ -109,10 +109,9 @@ def tile_groupedqueryattention_pa_k_kernel(
         stream[-1] = (proj, first_group, n_groups // 2)
         stream.append((proj, first_group + n_groups // 2, n_groups // 2))
 
-        load_scales(proj_q)
+        load_scales(proj_q, nc.gpsimd)
         chunks = [load_chunk(proj, first_group, n_groups) for proj, first_group, n_groups in stream[:CHUNK_BUFS]]
-        load_scales(proj_k)
-        load_scales(proj_v)
+        load_scales(proj_k, nc.gpsimd)
 
         x_codes = keep.tile([P, GROUPS * P], U32, name="x_codes", align_bytes=64)
         x_planes = keep.tile([P, GROUPS * P], U8, name="x_planes", align_bytes=64)
@@ -152,6 +151,8 @@ def tile_groupedqueryattention_pa_k_kernel(
                 quantise(waiting[0], waiting[1])
             waiting = (grouped, first_group)
         quantise(waiting[0], waiting[1])
+
+        load_scales(proj_v, nc.scalar)
 
         cos_pair = keep.tile([P, HALF, 2], F32, name="cos_pair")
         sin_minus = keep.tile([P, HALF], F32, name="sin_minus")

@@ -45,6 +45,7 @@ def tile_groupedqueryattention_pa_k_kernel(
         stage = ctx.enter_context(tc.tile_pool(name="stage", bufs=3))
         weights = ctx.enter_context(tc.tile_pool(name="weights", bufs=CHUNK_BUFS))
         work = ctx.enter_context(tc.tile_pool(name="work", bufs=2))
+        held = ctx.enter_context(tc.tile_pool(name="held", bufs=3))
         flip = ctx.enter_context(tc.psum_pool(name="flip", bufs=4))
         sums = ctx.enter_context(tc.psum_pool(name="sums", bufs=1))
 
@@ -161,7 +162,7 @@ def tile_groupedqueryattention_pa_k_kernel(
         nc.vector.tensor_copy(out=sin_plus[:], in_=sin_bf[:])
         nc.vector.tensor_scalar_mul(out=sin_minus[:], in0=sin_bf[:], scalar1=-1.0)
 
-        def rotate_and_store(bank, out_heads):
+        def rotate(bank, out_heads):
             heads = out_heads.shape[0]
             y = bank[:].rearrange("p (h q e) -> p h q e", h=heads, e=2)
             by_cos = work.tile([P, heads, D], F32, name="by_cos")
@@ -180,18 +181,22 @@ def tile_groupedqueryattention_pa_k_kernel(
                 out=by_sin[:, 1], in0=y[:, :, :, 0],
                 in1=sin_plus[:].unsqueeze(1).to_broadcast([P, heads, HALF]), op=MULT,
             )
-            rotated = work.tile([P, heads, HALF, 2], F32, name="rotated")
+            rotated = held.tile([P, heads, HALF, 2], F32, name="rotated")
             nc.vector.tensor_tensor(
                 out=rotated[:],
                 in0=by_cos[:].rearrange("p h (q e) -> p h q e", e=2),
                 in1=by_sin[:].rearrange("p e h q -> p h q e"),
                 op=ADD,
             )
-            nc.scalar.dma_start(
+            return (out_heads, rotated)
+
+        def store(out_heads, rotated):
+            nc.sync.dma_start(
                 out=out_heads.rearrange("h n d -> n h d"),
                 in_=rotated[:].rearrange("p h q e -> p h (q e)"),
             )
 
+        to_store = []
         for index, (proj, first_group, n_groups) in enumerate(stream):
             chunk = chunks[index]
             cols, width = proj["cols"], proj["width"]
@@ -210,13 +215,17 @@ def tile_groupedqueryattention_pa_k_kernel(
             if index + CHUNK_BUFS < len(stream):
                 later = stream[index + CHUNK_BUFS]
                 chunks.append(load_chunk(later[0], later[1], later[2]))
+            if index + CHUNK_BUFS >= len(stream) - 1:
+                for out_heads, rotated in to_store:
+                    store(out_heads, rotated)
+                to_store = []
             if first_group + n_groups == GROUPS:
                 if proj is proj_q:
                     heads_a_bank = BANK // D
                     for b, bank in enumerate(proj["banks"]):
-                        rotate_and_store(bank, out_0[0, b * heads_a_bank : (b + 1) * heads_a_bank])
+                        to_store.append(rotate(bank, out_0[0, b * heads_a_bank : (b + 1) * heads_a_bank]))
                 elif proj is proj_k:
-                    rotate_and_store(proj["banks"][0], out_1[0])
+                    to_store.append(rotate(proj["banks"][0], out_1[0]))
                 else:
                     v_rows = work.tile([P, V_COLS], F32, name="v_rows")
                     nc.vector.tensor_copy(out=v_rows[:], in_=proj["banks"][0][:])

@@ -228,8 +228,8 @@ def tile_groupedqueryattention_pa_k_kernel(
                     to_store.append(rotate(proj["banks"][0], out_1[0]))
                 else:
                     v_rows = work.tile([P, V_COLS], F32, name="v_rows")
-                    nc.vector.tensor_copy(out=v_rows[:], in_=proj["banks"][0][:])
-                    nc.sync.dma_start(
+                    nc.scalar.copy(out=v_rows[:], in_=proj["banks"][0][:])
+                    nc.scalar.dma_start(
                         out=out_2[0].rearrange("h n d -> n h d"),
                         in_=v_rows[:].rearrange("p (h d) -> p h d", d=D),
                     )

@@ -58,6 +58,7 @@ def tile_groupedqueryattention_pa_k_kernel(
             ]
             return {
                 "words": words.rearrange("g p n t -> g p (n t)").bitcast(I32),
+                "words_f32": words.rearrange("g p n t -> g p (n t)").bitcast(F32),
                 "scales": scales.bitcast(F32),
                 "planes": planes,
                 "cols": cols,
@@ -94,12 +95,18 @@ def tile_groupedqueryattention_pa_k_kernel(
                         in_=proj["scales"][:, 4 * quadrant + r, :].rearrange("(a j) w -> j a w", j=PLANES),
                     )
 
-        def load_chunk(proj, first_group, n_groups):
+        def load_chunk(index, proj, first_group, n_groups):
             chunk = weights.tile([P, CHUNK_WORDS], I32, name="chunk", align_bytes=64)
-            nc.sync.dma_start(
-                out=chunk[:, : n_groups * proj["cols"]].rearrange("p (g w) -> p g w", g=n_groups),
-                in_=proj["words"][first_group : first_group + n_groups].rearrange("g p w -> p g w"),
-            )
+            if index % 2 == 0:
+                nc.sync.dma_start(
+                    out=chunk[:, : n_groups * proj["cols"]].rearrange("p (g w) -> p g w", g=n_groups),
+                    in_=proj["words"][first_group : first_group + n_groups].rearrange("g p w -> p g w"),
+                )
+            else:
+                nc.scalar.dma_start(
+                    out=chunk[:, : n_groups * proj["cols"]].bitcast(F32).rearrange("p (g w) -> p g w", g=n_groups),
+                    in_=proj["words_f32"][first_group : first_group + n_groups].rearrange("g p w -> p g w"),
+                )
             return chunk
 
         stream = []
@@ -111,8 +118,12 @@ def tile_groupedqueryattention_pa_k_kernel(
         stream.append((proj, first_group + n_groups // 2, n_groups // 2))
 
         load_scales(proj_q, nc.gpsimd)
-        chunks = [load_chunk(proj, first_group, n_groups) for proj, first_group, n_groups in stream[:CHUNK_BUFS]]
+        chunks = [
+            load_chunk(index, proj, first_group, n_groups)
+            for index, (proj, first_group, n_groups) in enumerate(stream[:CHUNK_BUFS])
+        ]
         load_scales(proj_k, nc.gpsimd)
+        load_scales(proj_v, nc.gpsimd)
 
         x_codes = keep.tile([P, GROUPS * P], U32, name="x_codes", align_bytes=64)
         x_planes = keep.tile([P, GROUPS * P], U8, name="x_planes", align_bytes=64)
@@ -130,8 +141,7 @@ def tile_groupedqueryattention_pa_k_kernel(
                         nc.tensor.transpose(
                             flipped[:, i, u, :], x_words[:, base + u : base + K_PASS // 2 : 2], identity[:]
                         )
-                copy = nc.vector.tensor_copy if half % 2 == 0 else nc.scalar.copy
-                copy(
+                nc.vector.tensor_copy(
                     out=grouped_words[:, 2 * half : 2 * half + 2, :, :],
                     in_=flipped[:].rearrange("p i u m -> p i m u"),
                 )
@@ -153,13 +163,11 @@ def tile_groupedqueryattention_pa_k_kernel(
             waiting = (grouped, first_group)
         quantise(waiting[0], waiting[1])
 
-        load_scales(proj_v, nc.scalar)
-
         cos_pair = keep.tile([P, HALF, 2], F32, name="cos_pair")
         sin_minus = keep.tile([P, HALF], F32, name="sin_minus")
         sin_plus = keep.tile([P, HALF], F32, name="sin_plus")
         nc.vector.tensor_copy(out=cos_pair[:], in_=cos_bf[:].unsqueeze(2).to_broadcast([P, HALF, 2]))
-        nc.vector.tensor_copy(out=sin_plus[:], in_=sin_bf[:])
+        nc.scalar.copy(out=sin_plus[:], in_=sin_bf[:])
         nc.vector.tensor_scalar_mul(out=sin_minus[:], in0=sin_bf[:], scalar1=-1.0)
 
         def rotate(bank, out_heads):
@@ -214,7 +222,7 @@ def tile_groupedqueryattention_pa_k_kernel(
                     )
             if index + CHUNK_BUFS < len(stream):
                 later = stream[index + CHUNK_BUFS]
-                chunks.append(load_chunk(later[0], later[1], later[2]))
+                chunks.append(load_chunk(index + CHUNK_BUFS, later[0], later[1], later[2]))
             if index + CHUNK_BUFS >= len(stream) - 1:
                 for out_heads, rotated in to_store:
                     store(out_heads, rotated)

from contextlib import ExitStack

import concourse.mybir as mybir
from concourse.masks import make_identity

F32 = mybir.dt.float32
BF16 = mybir.dt.bfloat16
I32 = mybir.dt.int32
U32 = mybir.dt.uint32
U8 = mybir.dt.uint8
FP8X4 = mybir.dt.float8_e4m3fn_x4
MULT = mybir.AluOpType.mult
ADD = mybir.AluOpType.add

P = 128
E = 16384
K_PASS = 512
GROUPS = E // K_PASS
D = 128
HALF = D // 2
Q_COLS, K_COLS, V_COLS = 1024, 256, 256
BANK = 512
PLANES = 4

CHUNK_WORDS = 2048
MAX_RUNS = 4
CHUNK_BUFS = 16
X_CHUNKS = 4
X_CHUNK_GROUPS = GROUPS // X_CHUNKS
QUANT_GROUPS = 4

FLOPS = 2 * P * E * (Q_COLS + K_COLS + V_COLS)


def tile_groupedqueryattention_pa_k_kernel(
    tc, x, rope_cos, rope_sin,
    Wq_words, Wq_scales, Wk_words, Wk_scales, Wv_words, Wv_scales,
    out_0, out_1, out_2,
):
    nc = tc.nc
    with ExitStack() as ctx:
        ctx.enter_context(tc.manual_schedule())
        keep = ctx.enter_context(tc.tile_pool(name="keep", bufs=1))
        x_in = ctx.enter_context(tc.tile_pool(name="x_in", bufs=X_CHUNKS))
        stage = ctx.enter_context(tc.tile_pool(name="stage", bufs=3))
        weights = ctx.enter_context(tc.tile_pool(name="weights", bufs=CHUNK_BUFS))
        work = ctx.enter_context(tc.tile_pool(name="work", bufs=2))
        held = ctx.enter_context(tc.tile_pool(name="held", bufs=3))
        flip = ctx.enter_context(tc.psum_pool(name="flip", bufs=4))
        sums = ctx.enter_context(tc.psum_pool(name="sums", bufs=1))

        def projection(name, words, scales, cols):
            planes = keep.tile([P, GROUPS // PLANES, cols], U8, name=name + "_planes", align_bytes=64)
            nc.vector.memset(planes[:].bitcast(I32), 0)
            width = min(cols, BANK)
            banks = [
                sums.tile([P, width], F32, name="%s_sum%d" % (name, b)) for b in range(cols // width)
            ]
            return {
                "words": words.rearrange("g p n t -> g p (n t)").bitcast(I32),
                "words_f32": words.rearrange("g p n t -> g p (n t)").bitcast(F32),
                "scales": scales.bitcast(F32),
                "planes": planes,
                "cols": cols,
                "width": width,
                "banks": banks,
                "groups_per_chunk": min(CHUNK_WORDS // cols, MAX_RUNS),
            }

        proj_q = projection("q", Wq_words, Wq_scales, Q_COLS)
        proj_k = projection("k", Wk_words, Wk_scales, K_COLS)
        proj_v = projection("v", Wv_words, Wv_scales, V_COLS)

        identity = keep.tile([P, P], F32, name="identity")
        make_identity(nc, identity[:])

        x_tiles = []
        for c in range(X_CHUNKS):
            x_tile = x_in.tile([P, E // X_CHUNKS], BF16, name="x_tile")
            nc.sync.dma_start(out=x_tile[:], in_=x[0, :, c * (E // X_CHUNKS) : (c + 1) * (E // X_CHUNKS)])
            x_tiles.append(x_tile)

        cos_bf = keep.tile([P, HALF], BF16, name="cos_bf")
        sin_bf = keep.tile([P, HALF], BF16, name="sin_bf")
        nc.scalar.dma_start(out=cos_bf[:], in_=rope_cos[0])
        nc.scalar.dma_start(out=sin_bf[:], in_=rope_sin[0])

        def load_scales(proj, queue):
            plane_words = proj["planes"][:].bitcast(F32)
            for quadrant in range(4):
                for r in range(4):
                    first = 32 * quadrant + r
                    queue.dma_start(
                        out=plane_words[first : first + 4 * PLANES : 4, :, :],
                        in_=proj["scales"][:, 4 * quadrant + r, :].rearrange("(a j) w -> j a w", j=PLANES),
                    )

        def load_chunk(index, proj, first_group, n_groups):
            chunk = weights.tile([P, CHUNK_WORDS], I32, name="chunk", align_bytes=64)
            if index % 2 == 0:
                nc.sync.dma_start(
                    out=chunk[:, : n_groups * proj["cols"]].rearrange("p (g w) -> p g w", g=n_groups),
                    in_=proj["words"][first_group : first_group + n_groups].rearrange("g p w -> p g w"),
                )
            else:
                nc.scalar.dma_start(
                    out=chunk[:, : n_groups * proj["cols"]].bitcast(F32).rearrange("p (g w) -> p g w", g=n_groups),
                    in_=proj["words_f32"][first_group : first_group + n_groups].rearrange("g p w -> p g w"),
                )
            return chunk

        stream = []
        for proj in (proj_q, proj_k, proj_v):
            for first_group in range(0, GROUPS, proj["groups_per_chunk"]):
                stream.append((proj, first_group, proj["groups_per_chunk"]))
        proj, first_group, n_groups = stream[-1]
        stream[-1] = (proj, first_group, n_groups // 2)
        stream.append((proj, first_group + n_groups // 2, n_groups // 2))

        load_scales(proj_q, nc.gpsimd)
        chunks = [
            load_chunk(index, proj, first_group, n_groups)
            for index, (proj, first_group, n_groups) in enumerate(stream[:CHUNK_BUFS])
        ]
        load_scales(proj_k, nc.gpsimd)
        load_scales(proj_v, nc.gpsimd)

        x_codes = keep.tile([P, GROUPS * P], U32, name="x_codes", align_bytes=64)
        x_planes = keep.tile([P, GROUPS * P], U8, name="x_planes", align_bytes=64)

        def regroup(first_group):
            grouped = stage.tile([P, QUANT_GROUPS, P, 4], BF16, name="grouped", align_bytes=64)
            grouped_words = grouped[:].bitcast(F32)
            for half in range(QUANT_GROUPS // 2):
                flipped = flip.tile([P, 2, 2, P], F32, name="flipped")
                for i in range(2):
                    g = first_group + 2 * half + i
                    x_words = x_tiles[g // X_CHUNK_GROUPS][:].bitcast(F32)
                    base = (K_PASS // 2) * (g % X_CHUNK_GROUPS)
                    for u in range(2):
                        nc.tensor.transpose(
                            flipped[:, i, u, :], x_words[:, base + u : base + K_PASS // 2 : 2], identity[:]
                        )
                nc.vector.tensor_copy(
                    out=grouped_words[:, 2 * half : 2 * half + 2, :, :],
                    in_=flipped[:].rearrange("p i u m -> p i m u"),
                )
            return grouped

        def quantise(grouped, first_group):
            cols = slice(first_group * P, (first_group + QUANT_GROUPS) * P)
            nc.vector.quantize_mx(
                out=x_codes[:, cols].bitcast(FP8X4),
                scales=x_planes[:, cols],
                in_=grouped[:].rearrange("p g m t -> p (g m t)"),
            )

        waiting = None
        for first_group in range(0, GROUPS, QUANT_GROUPS):
            grouped = regroup(first_group)
            if waiting is not None:
                quantise(waiting[0], waiting[1])
            waiting = (grouped, first_group)
        quantise(waiting[0], waiting[1])

        cos_pair = keep.tile([P, HALF, 2], F32, name="cos_pair")
        sin_minus = keep.tile([P, HALF], F32, name="sin_minus")
        sin_plus = keep.tile([P, HALF], F32, name="sin_plus")
        nc.vector.tensor_copy(out=cos_pair[:], in_=cos_bf[:].unsqueeze(2).to_broadcast([P, HALF, 2]))
        nc.scalar.copy(out=sin_plus[:], in_=sin_bf[:])
        nc.vector.tensor_scalar_mul(out=sin_minus[:], in0=sin_bf[:], scalar1=-1.0)

        def rotate(bank, out_heads):
            heads = out_heads.shape[0]
            y = bank[:].rearrange("p (h q e) -> p h q e", h=heads, e=2)
            by_cos = work.tile([P, heads, D], F32, name="by_cos")
            nc.vector.tensor_tensor(
                out=by_cos[:],
                in0=bank[:].rearrange("p (h d) -> p h d", h=heads),
                in1=cos_pair[:].rearrange("p q e -> p (q e)").unsqueeze(1).to_broadcast([P, heads, D]),
                op=MULT,
            )
            by_sin = work.tile([P, 2, heads, HALF], F32, name="by_sin")
            nc.vector.tensor_tensor(
                out=by_sin[:, 0], in0=y[:, :, :, 1],
                in1=sin_minus[:].unsqueeze(1).to_broadcast([P, heads, HALF]), op=MULT,
            )
            nc.vector.tensor_tensor(
                out=by_sin[:, 1], in0=y[:, :, :, 0],
                in1=sin_plus[:].unsqueeze(1).to_broadcast([P, heads, HALF]), op=MULT,
            )
            rotated = held.tile([P, heads, HALF, 2], F32, name="rotated")
            nc.vector.tensor_tensor(
                out=rotated[:],
                in0=by_cos[:].rearrange("p h (q e) -> p h q e", e=2),
                in1=by_sin[:].rearrange("p e h q -> p h q e"),
                op=ADD,
            )
            return (out_heads, rotated)

        def store(out_heads, rotated):
            nc.sync.dma_start(
                out=out_heads.rearrange("h n d -> n h d"),
                in_=rotated[:].rearrange("p h q e -> p h (q e)"),
            )

        to_store = []
        for index, (proj, first_group, n_groups) in enumerate(stream):
            chunk = chunks[index]
            cols, width = proj["cols"], proj["width"]
            for i in range(n_groups):
                g = first_group + i
                for b, bank in enumerate(proj["banks"]):
                    nc.tensor.matmul_mx(
                        out=bank[:],
                        lhsT=x_codes[:, g * P : (g + 1) * P].bitcast(FP8X4),
                        lhsT_scale=x_planes[:, g * P : (g + 1) * P],
                        rhs=chunk[:, i * cols + b * width : i * cols + (b + 1) * width].bitcast(FP8X4),
                        rhs_scale=proj["planes"][4 * (g % PLANES) : P, g // PLANES, b * width : (b + 1) * width],
                        start=(g == 0),
                        stop=(g == GROUPS - 1),
                    )
            if index + CHUNK_BUFS < len(stream):
                later = stream[index + CHUNK_BUFS]
                chunks.append(load_chunk(index + CHUNK_BUFS, later[0], later[1], later[2]))
            if index + CHUNK_BUFS >= len(stream) - 1:
                for out_heads, rotated in to_store:
                    store(out_heads, rotated)
                to_store = []
            if first_group + n_groups == GROUPS:
                if proj is proj_q:
                    heads_a_bank = BANK // D
                    for b, bank in enumerate(proj["banks"]):
                        to_store.append(rotate(bank, out_0[0, b * heads_a_bank : (b + 1) * heads_a_bank]))
                elif proj is proj_k:
                    to_store.append(rotate(proj["banks"][0], out_1[0]))
                else:
                    v_rows = work.tile([P, V_COLS], F32, name="v_rows")
                    nc.scalar.copy(out=v_rows[:], in_=proj["banks"][0][:])
                    nc.scalar.dma_start(
                        out=out_2[0].rearrange("h n d -> n h d"),
                        in_=v_rows[:].rearrange("p (h d) -> p h d", d=D),
                    )
